import numpy as np
import ml_dtypes


def mxq(x, axis, fmt="e4m3"):
    dtype, down = {"e4m3": (ml_dtypes.float8_e4m3fn, 7), "e5m2": (ml_dtypes.float8_e5m2, 14)}[fmt]
    v = np.moveaxis(np.asarray(x, np.float32).astype(ml_dtypes.bfloat16).astype(np.float64), axis, -1)
    blocks = v.reshape(v.shape[:-1] + (-1, 32))
    amax = np.abs(blocks).max(-1, keepdims=True)
    byte = np.maximum(np.where(amax > 0, np.frexp(amax)[1] - 1 + 127, 0) - down, 1)
    scale = np.exp2(byte - 127.0)
    codes = (blocks / scale).astype(np.float32).astype(dtype).astype(np.float64)
    return np.moveaxis((codes * scale).reshape(v.shape), -1, axis)


WIDE = False


def mx_kscale(k):
    if not WIDE:
        return np.ones(k)
    levels = np.array([10, -10, 5, -5, 0])
    a = np.random.permutation(np.resize(levels, k // 512 * 4)).reshape(k // 512, 4)
    idx = np.arange(k)
    return np.exp2(a[idx // 512, idx % 128 // 32])


BF16 = ml_dtypes.bfloat16


def bf(x):
    return np.asarray(x, np.float32).astype(BF16)


def f64(x):
    return np.asarray(x).astype(np.float64)


E2M1 = np.array([0.0, 0.5, 1.0, 1.5, 2.0, 3.0, 4.0, 6.0, -0.0, -0.5, -1.0, -1.5, -2.0, -3.0, -4.0, -6.0])


def pack_weight(w, fmt):
    k, n = w.shape
    w = f64(bf(w)).reshape(k // 32, 32, n)
    amax = np.abs(w).max(1)
    if fmt == "e4m3":
        byte = np.frexp(amax)[1] - 1 + 127 - 7
    else:
        mant, ex = np.frexp(amax / 6.0)
        byte = np.where(mant > 0.5, ex, ex - 1) + 127
    byte = np.clip(np.where(amax > 0, byte, 1), 1, 254)
    scaled = (w * np.exp2(127.0 - byte)[:, None, :]).reshape(k, n).astype(np.float32)
    by_word = np.ascontiguousarray(scaled.reshape(k // 512, 128, 4, n).transpose(0, 1, 3, 2))
    if fmt == "e4m3":
        words = by_word.astype(ml_dtypes.float8_e4m3fn).view(np.uint8)
    else:
        c = by_word.astype(ml_dtypes.float4_e2m1fn).view(np.uint8) & 0xF
        words = c[..., 0::2] | (c[..., 1::2] << 4)
    return np.ascontiguousarray(words), np.ascontiguousarray(byte.astype(np.uint8).reshape(k // 512, 16, n))


def unpack_weight(words, scales, fmt):
    g, p, n, _ = words.shape
    if fmt == "e4m3":
        vals = np.ascontiguousarray(words).view(ml_dtypes.float8_e4m3fn).astype(np.float64)
    else:
        nib = np.empty((g, p, n, 4), np.uint8)
        nib[..., 0::2] = words & 0xF
        nib[..., 1::2] = words >> 4
        vals = E2M1[nib]
    vals = vals * np.repeat(np.exp2(scales.astype(np.float64) - 127.0), 8, axis=1)[..., None]
    return vals.transpose(0, 1, 3, 2).reshape(g * 512, n)


B, L, D = 3, 512, 512
SIG = 2.0
FMT = "e4m3"


def setup_inputs():
    s, t = mx_kscale(D), mx_kscale(D)
    x1 = bf(np.random.standard_normal((B, L, D)) * s)
    words, scales = pack_weight(np.random.standard_normal((D, D)) * SIG / D / s[:, None] * t, FMT)
    x2 = bf(np.random.standard_normal((B, L, D)) / t)
    return {"x1": x1,
            "bi_linear_w_words": words,
            "bi_linear_w_scales": scales,
            "x2": x2}


def reference(x1, bi_linear_w_words, bi_linear_w_scales, x2):
    h = mxq(f64(x1), 2, "e4m3") @ unpack_weight(bi_linear_w_words, bi_linear_w_scales, FMT)
    return mxq(h, 2, "e4m3") @ mxq(f64(x2), 2, "e4m3").transpose(0, 2, 1)

@@ -1,0 +1,152 @@
+from contextlib import ExitStack
+
+import concourse.mybir as mybir
+from concourse.masks import make_identity
+
+BF16 = mybir.dt.bfloat16
+F32 = mybir.dt.float32
+I32 = mybir.dt.int32
+U32 = mybir.dt.uint32
+U8 = mybir.dt.uint8
+FP8X4 = mybir.dt.float8_e4m3fn_x4
+
+B, L, D = 3, 512, 512
+P = 128
+PACK = 4
+CHUNKS = L // P
+HALF = L // 2
+
+FLOPS = 2 * B * L * D * D + 2 * B * L * L * D
+
+
+def copy_out_of_psum(nc, bank_index, out, in_):
+    if bank_index == 0:
+        nc.vector.tensor_copy(out=out, in_=in_)
+    else:
+        nc.scalar.copy(out=out, in_=in_)
+
+
+def quantise(nc, pool, operand, grouped):
+    codes = pool.tile([P, L], U32, align_bytes=64, tag=operand + "_codes")
+    scales = pool.tile([P, L], U8, align_bytes=64, tag=operand + "_scales")
+    nc.vector.quantize_mx(
+        out=codes[:].bitcast(FP8X4),
+        scales=scales[:],
+        in_=grouped[:].rearrange("p l s -> p (l s)"),
+    )
+    return codes, scales
+
+
+def tile_coattentionandcombine_pa_kernel(
+    tc, x1, bi_linear_w_words, bi_linear_w_scales, x2, out
+):
+    nc = tc.nc
+    with ExitStack() as ctx:
+        fixed = ctx.enter_context(tc.tile_pool(name="fixed", bufs=1))
+        per_batch = ctx.enter_context(tc.tile_pool(name="per_batch", bufs=B))
+        psum = ctx.enter_context(tc.psum_pool(name="psum", bufs=2))
+
+        w_scales = fixed.tile([P, D], U8, align_bytes=64)
+        nc.vector.memset(w_scales[:].bitcast(I32), 0)
+        ident_f32 = fixed.tile([P, P], F32)
+        make_identity(nc, ident_f32[:])
+        ident_bf16 = fixed.tile([P, P], BF16)
+        make_identity(nc, ident_bf16[:])
+
+        x1_rows = []
+        x2_half_rows = []
+        w_codes = fixed.tile([P, D], U32, align_bytes=64)
+        for b in range(B):
+            rows = per_batch.tile([P, CHUNKS, D], BF16)
+            nc.sync.dma_start(out=rows[:], in_=x1[b].rearrange("(p a) d -> p a d", a=CHUNKS))
+            x1_rows.append(rows)
+            if b == 0:
+                for q in range(4):
+                    nc.sync.dma_start(
+                        out=w_scales[32 * q : 32 * q + 4, :].bitcast(I32),
+                        in_=bi_linear_w_scales[0, 4 * q : 4 * q + 4, :].bitcast(I32),
+                    )
+                nc.sync.dma_start(
+                    out=w_codes[:].bitcast(I32),
+                    in_=bi_linear_w_words[0].rearrange("p n t -> p (n t)").bitcast(I32),
+                )
+            half_rows = per_batch.tile([P, L // 64, D // 2], BF16)
+            nc.sync.dma_start(
+                out=half_rows[:],
+                in_=x2[b].rearrange("(i r) (t c) -> (r t) i c", r=64, t=2),
+            )
+            x2_half_rows.append(half_rows)
+
+        for b in range(B):
+            x1_grouped = per_batch.tile([P, L, PACK], BF16, align_bytes=64)
+            for half in range(2):
+                x1_t = psum.tile([P, 2, HALF], F32)
+                for a in range(2):
+                    words = x1_rows[b][:, 2 * half + a, :].bitcast(F32)
+                    for u in range(2):
+                        nc.tensor.transpose(
+                            x1_t[:, u, P * a : P * (a + 1)], words[:, u : D // 2 : 2], ident_f32[:]
+                        )
+                copy_out_of_psum(
+                    nc,
+                    half,
+                    out=x1_grouped[:, HALF * half : HALF * (half + 1), :].bitcast(F32),
+                    in_=x1_t[:].rearrange("p u l -> p l u"),
+                )
+            x1_codes, x1_scales = quantise(nc, per_batch, "x1", x1_grouped)
+
+            h_grouped = per_batch.tile([P, L, PACK], BF16, align_bytes=64)
+            for a in range(CHUNKS):
+                cols = slice(P * a, P * (a + 1))
+                h_t = psum.tile([P, PACK, P], F32)
+                for s in range(PACK):
+                    n_cols = slice(256 * (s % 2) + P * (s // 2), 256 * (s % 2) + P * (s // 2) + P)
+                    nc.tensor.matmul_mx(
+                        out=h_t[:, s, :],
+                        lhsT=w_codes[:, n_cols].bitcast(FP8X4),
+                        lhsT_scale=w_scales[:, n_cols],
+                        rhs=x1_codes[:, cols].bitcast(FP8X4),
+                        rhs_scale=x1_scales[:, cols],
+                        start=True,
+                        stop=True,
+                    )
+                copy_out_of_psum(
+                    nc, a, out=h_grouped[:, cols, :], in_=h_t[:].rearrange("p s l -> p l s")
+                )
+            h_codes, h_scales = quantise(nc, per_batch, "h", h_grouped)
+
+            x2_grouped = per_batch.tile([P, L, PACK], BF16, align_bytes=64)
+            for half in range(2):
+                x2_t = psum.tile([P, 2, 2 * HALF], BF16)
+                for i in range(4):
+                    for v in range(2):
+                        nc.tensor.transpose(
+                            x2_t[:, v, P * i : P * (i + 1)],
+                            x2_half_rows[b][:, 4 * half + i, P * v : P * (v + 1)],
+                            ident_bf16[:],
+                        )
+                copy_out_of_psum(
+                    nc,
+                    half,
+                    out=x2_grouped[:, HALF * half : HALF * (half + 1), :].bitcast(F32),
+                    in_=x2_t[:].bitcast(F32).rearrange("p v l -> p l v"),
+                )
+            x2_codes, x2_scales = quantise(nc, per_batch, "x2", x2_grouped)
+
+            sim_rows = per_batch.tile([P, CHUNKS, L], F32)
+            out_rows = out[b].rearrange("(p a) m -> p a m", a=CHUNKS)
+            for a in range(CHUNKS):
+                cols = slice(P * a, P * (a + 1))
+                sim_bank = psum.tile([P, L], F32)
+                nc.tensor.matmul_mx(
+                    out=sim_bank[:],
+                    lhsT=h_codes[:, cols].bitcast(FP8X4),
+                    lhsT_scale=h_scales[:, cols],
+                    rhs=x2_codes[:].bitcast(FP8X4),
+                    rhs_scale=x2_scales[:],
+                    start=True,
+                    stop=True,
+                )
+                copy_out_of_psum(nc, a, out=sim_rows[:, a, :], in_=sim_bank[:])
+                if a % 2 == 1:
+                    nc.sync.dma_start(out=out_rows[:, a - 1 : a + 1, :], in_=sim_rows[:, a - 1 : a + 1, :])

@@ -19,24 +19,6 @@ HALF = L // 2
 FLOPS = 2 * B * L * D * D + 2 * B * L * L * D
 
 
-def copy_out_of_psum(nc, bank_index, out, in_):
-    if bank_index == 0:
-        nc.vector.tensor_copy(out=out, in_=in_)
-    else:
-        nc.scalar.copy(out=out, in_=in_)
-
-
-def quantise(nc, pool, operand, grouped):
-    codes = pool.tile([P, L], U32, align_bytes=64, tag=operand + "_codes")
-    scales = pool.tile([P, L], U8, align_bytes=64, tag=operand + "_scales")
-    nc.vector.quantize_mx(
-        out=codes[:].bitcast(FP8X4),
-        scales=scales[:],
-        in_=grouped[:].rearrange("p l s -> p (l s)"),
-    )
-    return codes, scales
-
-
 def tile_coattentionandcombine_pa_kernel(
     tc, x1, bi_linear_w_words, bi_linear_w_scales, x2, out
 ):
@@ -44,80 +26,99 @@ def tile_coattentionandcombine_pa_kernel(
     with ExitStack() as ctx:
         fixed = ctx.enter_context(tc.tile_pool(name="fixed", bufs=1))
         per_batch = ctx.enter_context(tc.tile_pool(name="per_batch", bufs=B))
-        psum = ctx.enter_context(tc.psum_pool(name="psum", bufs=2))
+        transposed = ctx.enter_context(tc.psum_pool(name="transposed", bufs=3))
+        products = ctx.enter_context(tc.psum_pool(name="products", bufs=5))
+        ctx.enter_context(tc.manual_schedule())
+
+        def copy_out_of_psum(bank_index, out_, in_):
+            if bank_index == 1:
+                nc.vector.tensor_copy(out=out_, in_=in_)
+            else:
+                nc.scalar.copy(out=out_, in_=in_)
+
+        def quantise(operand, cols):
+            grouped, codes, scales = operand
+            nc.vector.quantize_mx(
+                out=codes[:, cols].bitcast(FP8X4),
+                scales=scales[:, cols],
+                in_=grouped[:, cols, :].rearrange("p l s -> p (l s)"),
+            )
 
         w_scales = fixed.tile([P, D], U8, align_bytes=64)
         nc.vector.memset(w_scales[:].bitcast(I32), 0)
+        w_codes = fixed.tile([P, D], U32, align_bytes=64)
         ident_f32 = fixed.tile([P, P], F32)
         make_identity(nc, ident_f32[:])
         ident_bf16 = fixed.tile([P, P], BF16)
         make_identity(nc, ident_bf16[:])
 
-        x1_rows = []
-        x2_half_rows = []
-        w_codes = fixed.tile([P, D], U32, align_bytes=64)
+        x1_rows, x2_half_rows, x1_q, x2_q, h_q, sim_rows = [], [], [], [], [], []
         for b in range(B):
-            rows = per_batch.tile([P, CHUNKS, D], BF16)
-            nc.sync.dma_start(out=rows[:], in_=x1[b].rearrange("(p a) d -> p a d", a=CHUNKS))
+            rows = per_batch.tile([P, CHUNKS, D], BF16, tag="x1_rows")
             x1_rows.append(rows)
-            if b == 0:
-                for q in range(4):
-                    nc.sync.dma_start(
-                        out=w_scales[32 * q : 32 * q + 4, :].bitcast(I32),
-                        in_=bi_linear_w_scales[0, 4 * q : 4 * q + 4, :].bitcast(I32),
-                    )
-                nc.sync.dma_start(
-                    out=w_codes[:].bitcast(I32),
-                    in_=bi_linear_w_words[0].rearrange("p n t -> p (n t)").bitcast(I32),
-                )
-            half_rows = per_batch.tile([P, L // 64, D // 2], BF16)
+            half_rows = per_batch.tile([P, L // 64, D // 2], BF16, tag="x2_half_rows")
+            x2_half_rows.append(half_rows)
+            for operand, name in ((x1_q, "x1"), (x2_q, "x2"), (h_q, "h")):
+                grouped = per_batch.tile([P, L, PACK], BF16, align_bytes=64, tag=name + "_grouped")
+                codes = per_batch.tile([P, L], U32, align_bytes=64, tag=name + "_codes")
+                scales = per_batch.tile([P, L], U8, align_bytes=64, tag=name + "_scales")
+                operand.append((grouped, codes, scales))
+            result = per_batch.tile([P, CHUNKS, L], F32, tag="sim_rows")
+            sim_rows.append(result)
+
+        def load_x1(b, pieces):
+            rows = x1[b].rearrange("(p a) d -> p a d", a=CHUNKS)
+            step = CHUNKS // pieces
+            for a in range(0, CHUNKS, step):
+                nc.sync.dma_start(out=x1_rows[b][:, a : a + step, :], in_=rows[:, a : a + step, :])
+
+        def load_x2(b):
             nc.sync.dma_start(
-                out=half_rows[:],
+                out=x2_half_rows[b][:],
                 in_=x2[b].rearrange("(i r) (t c) -> (r t) i c", r=64, t=2),
             )
-            x2_half_rows.append(half_rows)
 
-        for b in range(B):
-            x1_grouped = per_batch.tile([P, L, PACK], BF16, align_bytes=64)
+        load_x1(0, 2)
+        load_x1(1, 1)
+        for q in range(4):
+            nc.sync.dma_start(
+                out=w_scales[32 * q : 32 * q + 4, :].bitcast(I32),
+                in_=bi_linear_w_scales[0, 4 * q : 4 * q + 4, :].bitcast(I32),
+            )
+        nc.sync.dma_start(
+            out=w_codes[:].bitcast(I32),
+            in_=bi_linear_w_words[0].rearrange("p n t -> p (n t)").bitcast(I32),
+        )
+        load_x2(0)
+        load_x2(1)
+        load_x1(2, 1)
+        load_x2(2)
+
+        def transpose_x1(b):
+            banks = []
             for half in range(2):
-                x1_t = psum.tile([P, 2, HALF], F32)
+                x1_t = transposed.tile([P, 2, HALF], F32, tag="t")
                 for a in range(2):
                     words = x1_rows[b][:, 2 * half + a, :].bitcast(F32)
                     for u in range(2):
                         nc.tensor.transpose(
                             x1_t[:, u, P * a : P * (a + 1)], words[:, u : D // 2 : 2], ident_f32[:]
                         )
-                copy_out_of_psum(
-                    nc,
-                    half,
-                    out=x1_grouped[:, HALF * half : HALF * (half + 1), :].bitcast(F32),
-                    in_=x1_t[:].rearrange("p u l -> p l u"),
-                )
-            x1_codes, x1_scales = quantise(nc, per_batch, "x1", x1_grouped)
+                banks.append(x1_t)
+            return banks
 
-            h_grouped = per_batch.tile([P, L, PACK], BF16, align_bytes=64)
-            for a in range(CHUNKS):
-                cols = slice(P * a, P * (a + 1))
-                h_t = psum.tile([P, PACK, P], F32)
-                for s in range(PACK):
-                    n_cols = slice(256 * (s % 2) + P * (s // 2), 256 * (s % 2) + P * (s // 2) + P)
-                    nc.tensor.matmul_mx(
-                        out=h_t[:, s, :],
-                        lhsT=w_codes[:, n_cols].bitcast(FP8X4),
-                        lhsT_scale=w_scales[:, n_cols],
-                        rhs=x1_codes[:, cols].bitcast(FP8X4),
-                        rhs_scale=x1_scales[:, cols],
-                        start=True,
-                        stop=True,
-                    )
-                copy_out_of_psum(
-                    nc, a, out=h_grouped[:, cols, :], in_=h_t[:].rearrange("p s l -> p l s")
-                )
-            h_codes, h_scales = quantise(nc, per_batch, "h", h_grouped)
-
-            x2_grouped = per_batch.tile([P, L, PACK], BF16, align_bytes=64)
+        def copy_x1(b, banks):
             for half in range(2):
-                x2_t = psum.tile([P, 2, 2 * HALF], BF16)
+                copy_out_of_psum(
+                    half,
+                    x1_q[b][0][:, HALF * half : HALF * (half + 1), :].bitcast(F32),
+                    banks[half][:].rearrange("p u l -> p l u"),
+                )
+
+        def transpose_x2(b):
+            banks = []
+            for half in range(2):
+                x2_t = transposed.tile([P, 2, 2 * HALF], BF16, tag="t")
                 for i in range(4):
                     for v in range(2):
                         nc.tensor.transpose(
@@ -125,28 +126,105 @@ def tile_coattentionandcombine_pa_kernel(
                             x2_half_rows[b][:, 4 * half + i, P * v : P * (v + 1)],
                             ident_bf16[:],
                         )
-                copy_out_of_psum(
-                    nc,
-                    half,
-                    out=x2_grouped[:, HALF * half : HALF * (half + 1), :].bitcast(F32),
-                    in_=x2_t[:].bitcast(F32).rearrange("p v l -> p l v"),
-                )
-            x2_codes, x2_scales = quantise(nc, per_batch, "x2", x2_grouped)
+                banks.append(x2_t)
+            return banks
 
-            sim_rows = per_batch.tile([P, CHUNKS, L], F32)
-            out_rows = out[b].rearrange("(p a) m -> p a m", a=CHUNKS)
+        def copy_x2(b, banks):
+            for half in range(2):
+                copy_out_of_psum(
+                    half,
+                    x2_q[b][0][:, HALF * half : HALF * (half + 1), :].bitcast(F32),
+                    banks[half][:].bitcast(F32).rearrange("p v l -> p l v"),
+                )
+
+        def quantise_halves(operand):
+            for half in range(2):
+                quantise(operand, slice(HALF * half, HALF * (half + 1)))
+
+        def project(b):
+            banks = []
             for a in range(CHUNKS):
                 cols = slice(P * a, P * (a + 1))
-                sim_bank = psum.tile([P, L], F32)
+                h_t = products.tile([P, PACK, P], F32, tag="p")
+                for s in range(PACK):
+                    n_cols = slice(256 * (s % 2) + P * (s // 2), 256 * (s % 2) + P * (s // 2) + P)
+                    nc.tensor.matmul_mx(
+                        out=h_t[:, s, :],
+                        lhsT=w_codes[:, n_cols].bitcast(FP8X4),
+                        lhsT_scale=w_scales[:, n_cols],
+                        rhs=x1_q[b][1][:, cols].bitcast(FP8X4),
+                        rhs_scale=x1_q[b][2][:, cols],
+                        start=True,
+                        stop=True,
+                    )
+                banks.append(h_t)
+            return banks
+
+        def copy_h(b, banks):
+            for a in range(CHUNKS):
+                copy_out_of_psum(
+                    a,
+                    h_q[b][0][:, P * a : P * (a + 1), :],
+                    banks[a][:].rearrange("p s l -> p l s"),
+                )
+
+        def quantise_h(b):
+            for a in range(CHUNKS):
+                quantise(h_q[b], slice(P * a, P * (a + 1)))
+
+        def similarity(b):
+            banks = []
+            for a in range(CHUNKS):
+                cols = slice(P * a, P * (a + 1))
+                sim_bank = products.tile([P, L], F32, tag="p")
                 nc.tensor.matmul_mx(
                     out=sim_bank[:],
-                    lhsT=h_codes[:, cols].bitcast(FP8X4),
-                    lhsT_scale=h_scales[:, cols],
-                    rhs=x2_codes[:].bitcast(FP8X4),
-                    rhs_scale=x2_scales[:],
+                    lhsT=h_q[b][1][:, cols].bitcast(FP8X4),
+                    lhsT_scale=h_q[b][2][:, cols],
+                    rhs=x2_q[b][1][:].bitcast(FP8X4),
+                    rhs_scale=x2_q[b][2][:],
                     start=True,
                     stop=True,
                 )
-                copy_out_of_psum(nc, a, out=sim_rows[:, a, :], in_=sim_bank[:])
-                if a % 2 == 1:
-                    nc.sync.dma_start(out=out_rows[:, a - 1 : a + 1, :], in_=sim_rows[:, a - 1 : a + 1, :])
+                banks.append(sim_bank)
+            return banks
+
+        def copy_and_store_sim(b, banks):
+            out_rows = out[b].rearrange("(p a) m -> p a m", a=CHUNKS)
+            for a in range(CHUNKS):
+                copy_out_of_psum(a % 2 if b == B - 1 else a, sim_rows[b][:, a, :], banks[a][:])
+                nc.sync.dma_start(out=out_rows[:, a, :], in_=sim_rows[b][:, a, :])
+
+        banks = transpose_x1(0)
+        copy_x1(0, banks)
+        banks = transpose_x1(1)
+        quantise_halves(x1_q[0])
+        copy_x1(1, banks)
+        banks = project(0)
+        quantise_halves(x1_q[1])
+        copy_h(0, banks)
+        banks = transpose_x2(0)
+        quantise_h(0)
+        copy_x2(0, banks)
+        banks = project(1)
+        quantise_halves(x2_q[0])
+        copy_h(1, banks)
+        banks = transpose_x2(1)
+        quantise_h(1)
+        copy_x2(1, banks)
+        banks = similarity(0)
+        quantise_halves(x2_q[1])
+        copy_and_store_sim(0, banks)
+        banks = transpose_x1(2)
+        copy_x1(2, banks)
+        banks = similarity(1)
+        quantise_halves(x1_q[2])
+        copy_and_store_sim(1, banks)
+        banks = transpose_x2(2)
+        copy_x2(2, banks)
+        banks = project(2)
+        quantise_halves(x2_q[2])
+        copy_h(2, banks)
+        quantise_h(2)
+        banks = similarity(2)
+        copy_and_store_sim(2, banks)

@@ -15,6 +15,15 @@ P = 128
 PACK = 4
 CHUNKS = L // P
 HALF = L // 2
+HALVES = L // HALF
+PLANES = 2
+WORDS = D // 2
+PAIRED = P // 2
+QUADRANT = 32
+SCALE_ROWS = 4
+
+TRANSPOSE_BANKS = 3
+PRODUCT_BANKS = 5
 
 FLOPS = 2 * B * L * D * D + 2 * B * L * L * D
 
@@ -26,22 +35,21 @@ def tile_coattentionandcombine_pa_kernel(
     with ExitStack() as ctx:
         fixed = ctx.enter_context(tc.tile_pool(name="fixed", bufs=1))
         per_batch = ctx.enter_context(tc.tile_pool(name="per_batch", bufs=B))
-        transposed = ctx.enter_context(tc.psum_pool(name="transposed", bufs=3))
-        products = ctx.enter_context(tc.psum_pool(name="products", bufs=5))
+        transposed = ctx.enter_context(tc.psum_pool(name="transposed", bufs=TRANSPOSE_BANKS))
+        products = ctx.enter_context(tc.psum_pool(name="products", bufs=PRODUCT_BANKS))
         ctx.enter_context(tc.manual_schedule())
 
-        def copy_out_of_psum(bank_index, out_, in_):
-            if bank_index == 1:
+        def copy_out_of_psum(on_vector, out_, in_):
+            if on_vector:
                 nc.vector.tensor_copy(out=out_, in_=in_)
             else:
                 nc.scalar.copy(out=out_, in_=in_)
 
         def quantise(operand, cols):
-            grouped, codes, scales = operand
             nc.vector.quantize_mx(
-                out=codes[:, cols].bitcast(FP8X4),
-                scales=scales[:, cols],
-                in_=grouped[:, cols, :].rearrange("p l s -> p (l s)"),
+                out=operand["codes"][:, cols].bitcast(FP8X4),
+                scales=operand["scales"][:, cols],
+                in_=operand["grouped"][:, cols, :].rearrange("p l s -> p (l s)"),
             )
 
         w_scales = fixed.tile([P, D], U8, align_bytes=64)
@@ -56,13 +64,13 @@ def tile_coattentionandcombine_pa_kernel(
         for b in range(B):
             rows = per_batch.tile([P, CHUNKS, D], BF16, tag="x1_rows")
             x1_rows.append(rows)
-            half_rows = per_batch.tile([P, L // 64, D // 2], BF16, tag="x2_half_rows")
+            half_rows = per_batch.tile([P, L // PAIRED, D // 2], BF16, tag="x2_half_rows")
             x2_half_rows.append(half_rows)
-            for operand, name in ((x1_q, "x1"), (x2_q, "x2"), (h_q, "h")):
+            for operands, name in ((x1_q, "x1"), (x2_q, "x2"), (h_q, "h")):
                 grouped = per_batch.tile([P, L, PACK], BF16, align_bytes=64, tag=name + "_grouped")
                 codes = per_batch.tile([P, L], U32, align_bytes=64, tag=name + "_codes")
                 scales = per_batch.tile([P, L], U8, align_bytes=64, tag=name + "_scales")
-                operand.append((grouped, codes, scales))
+                operands.append({"grouped": grouped, "codes": codes, "scales": scales})
             result = per_batch.tile([P, CHUNKS, L], F32, tag="sim_rows")
             sim_rows.append(result)
 
@@ -75,15 +83,15 @@ def tile_coattentionandcombine_pa_kernel(
         def load_x2(b):
             nc.sync.dma_start(
                 out=x2_half_rows[b][:],
-                in_=x2[b].rearrange("(i r) (t c) -> (r t) i c", r=64, t=2),
+                in_=x2[b].rearrange("(i r) (t c) -> (r t) i c", r=PAIRED, t=2),
             )
 
-        load_x1(0, 2)
+        load_x1(0, HALVES)
         load_x1(1, 1)
-        for q in range(4):
+        for q in range(P // QUADRANT):
             nc.sync.dma_start(
-                out=w_scales[32 * q : 32 * q + 4, :].bitcast(I32),
-                in_=bi_linear_w_scales[0, 4 * q : 4 * q + 4, :].bitcast(I32),
+                out=w_scales[QUADRANT * q : QUADRANT * q + SCALE_ROWS, :].bitcast(I32),
+                in_=bi_linear_w_scales[0, SCALE_ROWS * q : SCALE_ROWS * (q + 1), :].bitcast(I32),
             )
         nc.sync.dma_start(
             out=w_codes[:].bitcast(I32),
@@ -94,52 +102,47 @@ def tile_coattentionandcombine_pa_kernel(
         load_x1(2, 1)
         load_x2(2)
 
-        def transpose_x1(b):
+
+        def prepare_x1(b):
             banks = []
-            for half in range(2):
-                x1_t = transposed.tile([P, 2, HALF], F32, tag="t")
-                for a in range(2):
-                    words = x1_rows[b][:, 2 * half + a, :].bitcast(F32)
-                    for u in range(2):
+            for half in range(HALVES):
+                x1_t = transposed.tile([P, PLANES, HALF], F32, tag="t")
+                for a in range(HALF // P):
+                    words = x1_rows[b][:, HALF // P * half + a, :].bitcast(F32)
+                    for u in range(PLANES):
                         nc.tensor.transpose(
-                            x1_t[:, u, P * a : P * (a + 1)], words[:, u : D // 2 : 2], ident_f32[:]
+                            x1_t[:, u, P * a : P * (a + 1)], words[:, u:WORDS:PLANES], ident_f32[:]
                         )
                 banks.append(x1_t)
-            return banks
-
-        def copy_x1(b, banks):
-            for half in range(2):
+            for half in range(HALVES):
                 copy_out_of_psum(
-                    half,
-                    x1_q[b][0][:, HALF * half : HALF * (half + 1), :].bitcast(F32),
+                    half == 1,
+                    x1_q[b]["grouped"][:, HALF * half : HALF * (half + 1), :].bitcast(F32),
                     banks[half][:].rearrange("p u l -> p l u"),
                 )
+            for half in range(HALVES):
+                quantise(x1_q[b], slice(HALF * half, HALF * (half + 1)))
 
-        def transpose_x2(b):
+        def prepare_x2(b):
             banks = []
-            for half in range(2):
-                x2_t = transposed.tile([P, 2, 2 * HALF], BF16, tag="t")
-                for i in range(4):
-                    for v in range(2):
+            for half in range(HALVES):
+                x2_t = transposed.tile([P, PLANES, 2 * HALF], BF16, tag="t")
+                for i in range(HALF // PAIRED):
+                    for v in range(PLANES):
                         nc.tensor.transpose(
                             x2_t[:, v, P * i : P * (i + 1)],
-                            x2_half_rows[b][:, 4 * half + i, P * v : P * (v + 1)],
+                            x2_half_rows[b][:, HALF // PAIRED * half + i, P * v : P * (v + 1)],
                             ident_bf16[:],
                         )
                 banks.append(x2_t)
-            return banks
-
-        def copy_x2(b, banks):
-            for half in range(2):
+            for half in range(HALVES):
                 copy_out_of_psum(
-                    half,
-                    x2_q[b][0][:, HALF * half : HALF * (half + 1), :].bitcast(F32),
+                    half == 1,
+                    x2_q[b]["grouped"][:, HALF * half : HALF * (half + 1), :].bitcast(F32),
                     banks[half][:].bitcast(F32).rearrange("p v l -> p l v"),
                 )
-
-        def quantise_halves(operand):
-            for half in range(2):
-                quantise(operand, slice(HALF * half, HALF * (half + 1)))
+            for half in range(HALVES):
+                quantise(x2_q[b], slice(HALF * half, HALF * (half + 1)))
 
         def project(b):
             banks = []
@@ -147,28 +150,24 @@ def tile_coattentionandcombine_pa_kernel(
                 cols = slice(P * a, P * (a + 1))
                 h_t = products.tile([P, PACK, P], F32, tag="p")
                 for s in range(PACK):
-                    n_cols = slice(256 * (s % 2) + P * (s // 2), 256 * (s % 2) + P * (s // 2) + P)
+                    first = D // 2 * (s % 2) + P * (s // 2)
+                    n_cols = slice(first, first + P)
                     nc.tensor.matmul_mx(
                         out=h_t[:, s, :],
                         lhsT=w_codes[:, n_cols].bitcast(FP8X4),
                         lhsT_scale=w_scales[:, n_cols],
-                        rhs=x1_q[b][1][:, cols].bitcast(FP8X4),
-                        rhs_scale=x1_q[b][2][:, cols],
+                        rhs=x1_q[b]["codes"][:, cols].bitcast(FP8X4),
+                        rhs_scale=x1_q[b]["scales"][:, cols],
                         start=True,
                         stop=True,
                     )
                 banks.append(h_t)
-            return banks
-
-        def copy_h(b, banks):
             for a in range(CHUNKS):
                 copy_out_of_psum(
-                    a,
-                    h_q[b][0][:, P * a : P * (a + 1), :],
+                    a == 1,
+                    h_q[b]["grouped"][:, P * a : P * (a + 1), :],
                     banks[a][:].rearrange("p s l -> p l s"),
                 )
-
-        def quantise_h(b):
             for a in range(CHUNKS):
                 quantise(h_q[b], slice(P * a, P * (a + 1)))
 
@@ -179,52 +178,30 @@ def tile_coattentionandcombine_pa_kernel(
                 sim_bank = products.tile([P, L], F32, tag="p")
                 nc.tensor.matmul_mx(
                     out=sim_bank[:],
-                    lhsT=h_q[b][1][:, cols].bitcast(FP8X4),
-                    lhsT_scale=h_q[b][2][:, cols],
-                    rhs=x2_q[b][1][:].bitcast(FP8X4),
-                    rhs_scale=x2_q[b][2][:],
+                    lhsT=h_q[b]["codes"][:, cols].bitcast(FP8X4),
+                    lhsT_scale=h_q[b]["scales"][:, cols],
+                    rhs=x2_q[b]["codes"][:].bitcast(FP8X4),
+                    rhs_scale=x2_q[b]["scales"][:],
                     start=True,
                     stop=True,
                 )
                 banks.append(sim_bank)
-            return banks
-
-        def copy_and_store_sim(b, banks):
             out_rows = out[b].rearrange("(p a) m -> p a m", a=CHUNKS)
             for a in range(CHUNKS):
-                copy_out_of_psum(a % 2 if b == B - 1 else a, sim_rows[b][:, a, :], banks[a][:])
+                copy_out_of_psum(
+                    a % 2 == 1 if b == B - 1 else a == 1, sim_rows[b][:, a, :], banks[a][:]
+                )
                 nc.sync.dma_start(out=out_rows[:, a, :], in_=sim_rows[b][:, a, :])
 
-        banks = transpose_x1(0)
-        copy_x1(0, banks)
-        banks = transpose_x1(1)
-        quantise_halves(x1_q[0])
-        copy_x1(1, banks)
-        banks = project(0)
-        quantise_halves(x1_q[1])
-        copy_h(0, banks)
-        banks = transpose_x2(0)
-        quantise_h(0)
-        copy_x2(0, banks)
-        banks = project(1)
-        quantise_halves(x2_q[0])
-        copy_h(1, banks)
-        banks = transpose_x2(1)
-        quantise_h(1)
-        copy_x2(1, banks)
-        banks = similarity(0)
-        quantise_halves(x2_q[1])
-        copy_and_store_sim(0, banks)
-        banks = transpose_x1(2)
-        copy_x1(2, banks)
-        banks = similarity(1)
-        quantise_halves(x1_q[2])
-        copy_and_store_sim(1, banks)
-        banks = transpose_x2(2)
-        copy_x2(2, banks)
-        banks = project(2)
-        quantise_halves(x2_q[2])
-        copy_h(2, banks)
-        quantise_h(2)
-        banks = similarity(2)
-        copy_and_store_sim(2, banks)
+        prepare_x1(0)
+        prepare_x1(1)
+        project(0)
+        prepare_x2(0)
+        project(1)
+        prepare_x2(1)
+        similarity(0)
+        prepare_x1(2)
+        similarity(1)
+        prepare_x2(2)
+        project(2)
+        similarity(2)

from contextlib import ExitStack

import concourse.mybir as mybir
from concourse.masks import make_identity

BF16 = mybir.dt.bfloat16
F32 = mybir.dt.float32
I32 = mybir.dt.int32
U32 = mybir.dt.uint32
U8 = mybir.dt.uint8
FP8X4 = mybir.dt.float8_e4m3fn_x4

B, L, D = 3, 512, 512
P = 128
PACK = 4
CHUNKS = L // P
HALF = L // 2
HALVES = L // HALF
PLANES = 2
WORDS = D // 2
PAIRED = P // 2
QUADRANT = 32
SCALE_ROWS = 4

TRANSPOSE_BANKS = 3
PRODUCT_BANKS = 5

FLOPS = 2 * B * L * D * D + 2 * B * L * L * D


def tile_coattentionandcombine_pa_kernel(
    tc, x1, bi_linear_w_words, bi_linear_w_scales, x2, out
):
    nc = tc.nc
    with ExitStack() as ctx:
        fixed = ctx.enter_context(tc.tile_pool(name="fixed", bufs=1))
        per_batch = ctx.enter_context(tc.tile_pool(name="per_batch", bufs=B))
        transposed = ctx.enter_context(tc.psum_pool(name="transposed", bufs=TRANSPOSE_BANKS))
        products = ctx.enter_context(tc.psum_pool(name="products", bufs=PRODUCT_BANKS))
        ctx.enter_context(tc.manual_schedule())

        def copy_out_of_psum(on_vector, out_, in_):
            if on_vector:
                nc.vector.tensor_copy(out=out_, in_=in_)
            else:
                nc.scalar.copy(out=out_, in_=in_)

        def quantise(operand, cols):
            nc.vector.quantize_mx(
                out=operand["codes"][:, cols].bitcast(FP8X4),
                scales=operand["scales"][:, cols],
                in_=operand["grouped"][:, cols, :].rearrange("p l s -> p (l s)"),
            )

        w_scales = fixed.tile([P, D], U8, align_bytes=64)
        nc.vector.memset(w_scales[:].bitcast(I32), 0)
        w_codes = fixed.tile([P, D], U32, align_bytes=64)
        ident_f32 = fixed.tile([P, P], F32)
        make_identity(nc, ident_f32[:])
        ident_bf16 = fixed.tile([P, P], BF16)
        make_identity(nc, ident_bf16[:])

        x1_rows, x2_half_rows, x1_q, x2_q, h_q, sim_rows = [], [], [], [], [], []
        for b in range(B):
            rows = per_batch.tile([P, CHUNKS, D], BF16, tag="x1_rows")
            x1_rows.append(rows)
            half_rows = per_batch.tile([P, L // PAIRED, D // 2], BF16, tag="x2_half_rows")
            x2_half_rows.append(half_rows)
            for operands, name in ((x1_q, "x1"), (x2_q, "x2"), (h_q, "h")):
                grouped = per_batch.tile([P, L, PACK], BF16, align_bytes=64, tag=name + "_grouped")
                codes = per_batch.tile([P, L], U32, align_bytes=64, tag=name + "_codes")
                scales = per_batch.tile([P, L], U8, align_bytes=64, tag=name + "_scales")
                operands.append({"grouped": grouped, "codes": codes, "scales": scales})
            result = per_batch.tile([P, CHUNKS, L], F32, tag="sim_rows")
            sim_rows.append(result)

        def load_x1(b, pieces):
            rows = x1[b].rearrange("(p a) d -> p a d", a=CHUNKS)
            step = CHUNKS // pieces
            for a in range(0, CHUNKS, step):
                nc.sync.dma_start(out=x1_rows[b][:, a : a + step, :], in_=rows[:, a : a + step, :])

        def load_x2(b):
            nc.sync.dma_start(
                out=x2_half_rows[b][:],
                in_=x2[b].rearrange("(i r) (t c) -> (r t) i c", r=PAIRED, t=2),
            )

        load_x1(0, HALVES)
        load_x1(1, 1)
        for q in range(P // QUADRANT):
            nc.sync.dma_start(
                out=w_scales[QUADRANT * q : QUADRANT * q + SCALE_ROWS, :].bitcast(I32),
                in_=bi_linear_w_scales[0, SCALE_ROWS * q : SCALE_ROWS * (q + 1), :].bitcast(I32),
            )
        nc.sync.dma_start(
            out=w_codes[:].bitcast(I32),
            in_=bi_linear_w_words[0].rearrange("p n t -> p (n t)").bitcast(I32),
        )
        load_x2(0)
        load_x2(1)
        load_x1(2, 1)
        load_x2(2)


        def prepare_x1(b):
            banks = []
            for half in range(HALVES):
                x1_t = transposed.tile([P, PLANES, HALF], F32, tag="t")
                for a in range(HALF // P):
                    words = x1_rows[b][:, HALF // P * half + a, :].bitcast(F32)
                    for u in range(PLANES):
                        nc.tensor.transpose(
                            x1_t[:, u, P * a : P * (a + 1)], words[:, u:WORDS:PLANES], ident_f32[:]
                        )
                banks.append(x1_t)
            for half in range(HALVES):
                copy_out_of_psum(
                    half == 1,
                    x1_q[b]["grouped"][:, HALF * half : HALF * (half + 1), :].bitcast(F32),
                    banks[half][:].rearrange("p u l -> p l u"),
                )
            for half in range(HALVES):
                quantise(x1_q[b], slice(HALF * half, HALF * (half + 1)))

        def prepare_x2(b):
            banks = []
            for half in range(HALVES):
                x2_t = transposed.tile([P, PLANES, 2 * HALF], BF16, tag="t")
                for i in range(HALF // PAIRED):
                    for v in range(PLANES):
                        nc.tensor.transpose(
                            x2_t[:, v, P * i : P * (i + 1)],
                            x2_half_rows[b][:, HALF // PAIRED * half + i, P * v : P * (v + 1)],
                            ident_bf16[:],
                        )
                banks.append(x2_t)
            for half in range(HALVES):
                copy_out_of_psum(
                    half == 1,
                    x2_q[b]["grouped"][:, HALF * half : HALF * (half + 1), :].bitcast(F32),
                    banks[half][:].bitcast(F32).rearrange("p v l -> p l v"),
                )
            for half in range(HALVES):
                quantise(x2_q[b], slice(HALF * half, HALF * (half + 1)))

        def project(b):
            banks = []
            for a in range(CHUNKS):
                cols = slice(P * a, P * (a + 1))
                h_t = products.tile([P, PACK, P], F32, tag="p")
                for s in range(PACK):
                    first = D // 2 * (s % 2) + P * (s // 2)
                    n_cols = slice(first, first + P)
                    nc.tensor.matmul_mx(
                        out=h_t[:, s, :],
                        lhsT=w_codes[:, n_cols].bitcast(FP8X4),
                        lhsT_scale=w_scales[:, n_cols],
                        rhs=x1_q[b]["codes"][:, cols].bitcast(FP8X4),
                        rhs_scale=x1_q[b]["scales"][:, cols],
                        start=True,
                        stop=True,
                    )
                banks.append(h_t)
            for a in range(CHUNKS):
                copy_out_of_psum(
                    a == 1,
                    h_q[b]["grouped"][:, P * a : P * (a + 1), :],
                    banks[a][:].rearrange("p s l -> p l s"),
                )
            for a in range(CHUNKS):
                quantise(h_q[b], slice(P * a, P * (a + 1)))

        def similarity(b):
            banks = []
            for a in range(CHUNKS):
                cols = slice(P * a, P * (a + 1))
                sim_bank = products.tile([P, L], F32, tag="p")
                nc.tensor.matmul_mx(
                    out=sim_bank[:],
                    lhsT=h_q[b]["codes"][:, cols].bitcast(FP8X4),
                    lhsT_scale=h_q[b]["scales"][:, cols],
                    rhs=x2_q[b]["codes"][:].bitcast(FP8X4),
                    rhs_scale=x2_q[b]["scales"][:],
                    start=True,
                    stop=True,
                )
                banks.append(sim_bank)
            out_rows = out[b].rearrange("(p a) m -> p a m", a=CHUNKS)
            for a in range(CHUNKS):
                copy_out_of_psum(
                    a % 2 == 1 if b == B - 1 else a == 1, sim_rows[b][:, a, :], banks[a][:]
                )
                nc.sync.dma_start(out=out_rows[:, a, :], in_=sim_rows[b][:, a, :])

        prepare_x1(0)
        prepare_x1(1)
        project(0)
        prepare_x2(0)
        project(1)
        prepare_x2(1)
        similarity(0)
        prepare_x1(2)
        similarity(1)
        prepare_x2(2)
        project(2)
        similarity(2)
